import numpy as np
import ml_dtypes

BF16 = ml_dtypes.bfloat16


def bf(x):
    return np.asarray(x, np.float32).astype(BF16)


def f32(x):
    return np.asarray(x, np.float32)


def f64(x):
    return np.asarray(x).astype(np.float64)


def striped(idx):
    return np.tile(idx.reshape(-1, 16).T, (8, 1))


D, S, K, M, N, H = 128, 1024, 4, 256, 4096, 512
SLOPE = 0.2


def setup_inputs():
    x = bf(np.random.standard_normal((D, S)))
    wa = bf(np.random.standard_normal((D, M)) / np.sqrt(2.0 * D))
    wb = bf(np.random.standard_normal((D, M)) / np.sqrt(2.0 * D))
    b = f32(0.1 * np.random.standard_normal((M, 1)))
    idx = np.concatenate([np.random.permutation(S)[:H] for _ in range(N // H)])
    return {"x": x, "wa": wa, "wb": wb, "b": b, "offs": striped(idx)}


def reference(x, wa, wb, b, offs):
    idx = offs[:16].T.reshape(-1)
    xs = f64(x)
    nb = (f64(wa).T @ xs[:, idx]).reshape(M, K, S)
    ctr = f64(wb).T @ xs - f64(wa).T @ xs + f64(b)
    h = nb + ctr[:, None, :]
    return np.maximum(h, SLOPE * h).max(axis=1)

@@ -1,0 +1,73 @@
+import concourse.mybir as mybir
+
+BF16, F32, U16 = mybir.dt.bfloat16, mybir.dt.float32, mybir.dt.uint16
+ADD, MULT, MAX = mybir.AluOpType.add, mybir.AluOpType.mult, mybir.AluOpType.max
+
+P = 128
+NODES = 1024
+FEATURES = 256
+NEIGHBOURS = 4
+PIECE = 512
+SLOPE = 0.2
+
+FLOPS = 2 * P * FEATURES * (NEIGHBOURS * NODES + 2 * NODES)
+
+
+def tile_skeletonconv_kernel(tc, x, wa, wb, b, offs, out):
+    nc = tc.nc
+    blocks = FEATURES // P
+    halves = NODES // PIECE
+    cols = PIECE // 16
+
+    with (
+        tc.tile_pool(name="held", bufs=1) as held,
+        tc.tile_pool(name="work", bufs=2) as work,
+        tc.psum_pool(name="centres", bufs=1) as centres,
+        tc.psum_pool(name="products", bufs=4) as products,
+    ):
+        offsets = held.tile([P, NEIGHBOURS * NODES // 16], U16, name="offsets")
+        nc.sync.dma_start(offsets[:], offs)
+        nodes = held.tile([P, NODES], BF16, name="nodes")
+        nc.scalar.dma_start(nodes[:], x)
+        wb_sb = held.tile([P, FEATURES], BF16, name="wb_sb")
+        nc.gpsimd.dma_start(wb_sb[:], wb)
+        wa_sb = held.tile([P, FEATURES], BF16, name="wa_sb")
+        nc.gpsimd.dma_start(wa_sb[:], wa)
+        bias = [held.tile([P, 1], F32, name=f"bias{f}") for f in range(blocks)]
+        for f in range(blocks):
+            nc.sync.dma_start(bias[f][:], b[f * P : (f + 1) * P, :])
+
+        wa_neg = held.tile([P, FEATURES], BF16, name="wa_neg")
+        nc.vector.tensor_scalar_mul(wa_neg[:], wa_sb[:], -1.0)
+
+        centre = {}
+        for f in range(blocks):
+            for h in range(halves):
+                centre[f, h] = centres.tile([P, PIECE], F32, name=f"centre{f}{h}")
+                here = nodes[:, h * PIECE : (h + 1) * PIECE]
+                feats = slice(f * P, (f + 1) * P)
+                nc.tensor.matmul(centre[f, h][:], wb_sb[:, feats], here, start=True, stop=False)
+                nc.tensor.matmul(centre[f, h][:], wa_neg[:, feats], here, start=False, stop=True)
+
+        for f in range(blocks):
+            for h in range(halves):
+                best = work.tile([P, PIECE], F32, name="best")
+                for k in range(NEIGHBOURS):
+                    piece = k * halves + h
+                    product = products.tile([P, PIECE], F32, name="product")
+                    nc.tensor.matmul(
+                        product[:],
+                        wa_sb[:, f * P : (f + 1) * P],
+                        nodes[:].indirect(offsets[:, piece * cols : (piece + 1) * cols]),
+                        start=True,
+                        stop=True,
+                    )
+                    if k == 0:
+                        nc.scalar.copy(best[:], product[:])
+                    else:
+                        nc.vector.tensor_tensor(best[:], product[:], best[:], MAX)
+                summed = work.tile([P, PIECE], F32, name="summed")
+                nc.vector.scalar_tensor_tensor(summed[:], centre[f, h][:], bias[f][:], best[:], ADD, ADD)
+                result = work.tile([P, PIECE], F32, name="result")
+                nc.vector.scalar_tensor_tensor(result[:], summed[:], SLOPE, summed[:], MULT, MAX)
+                nc.sync.dma_start(out[f * P : (f + 1) * P, h * PIECE : (h + 1) * PIECE], result[:])

@@ -15,59 +15,56 @@ FLOPS = 2 * P * FEATURES * (NEIGHBOURS * NODES + 2 * NODES)
 
 def tile_skeletonconv_kernel(tc, x, wa, wb, b, offs, out):
     nc = tc.nc
-    blocks = FEATURES // P
-    halves = NODES // PIECE
     cols = PIECE // 16
+    halves = NODES // PIECE
+    units = [(f, h) for f in range(FEATURES // P) for h in range(halves)]
 
     with (
         tc.tile_pool(name="held", bufs=1) as held,
         tc.tile_pool(name="work", bufs=2) as work,
-        tc.psum_pool(name="centres", bufs=1) as centres,
-        tc.psum_pool(name="products", bufs=4) as products,
+        tc.psum_pool(name="psum", bufs=8) as psum,
     ):
         offsets = held.tile([P, NEIGHBOURS * NODES // 16], U16, name="offsets")
-        nc.sync.dma_start(offsets[:], offs)
         nodes = held.tile([P, NODES], BF16, name="nodes")
-        nc.scalar.dma_start(nodes[:], x)
         wb_sb = held.tile([P, FEATURES], BF16, name="wb_sb")
-        nc.gpsimd.dma_start(wb_sb[:], wb)
         wa_sb = held.tile([P, FEATURES], BF16, name="wa_sb")
-        nc.gpsimd.dma_start(wa_sb[:], wa)
-        bias = [held.tile([P, 1], F32, name=f"bias{f}") for f in range(blocks)]
-        for f in range(blocks):
-            nc.sync.dma_start(bias[f][:], b[f * P : (f + 1) * P, :])
+        bias = [held.tile([P, 1], F32, name=f"bias{f}") for f in range(FEATURES // P)]
+        nc.sync.dma_start(nodes[:], x)
+        nc.scalar.dma_start(wa_sb[:], wa)
+        nc.sync.dma_start(offsets[:], offs)
+        nc.scalar.dma_start(wb_sb[:], wb)
+        for f in range(FEATURES // P):
+            nc.scalar.dma_start(bias[f][:], b[f * P : (f + 1) * P, :])
+
+        best = {}
+        for f, h in units:
+            best[f, h] = held.tile([P, PIECE], F32, name=f"best{f}{h}")
+            for k in range(NEIGHBOURS):
+                piece = k * halves + h
+                product = psum.tile([P, PIECE], F32, name="product", tag="bank")
+                nc.tensor.matmul(
+                    product[:],
+                    wa_sb[:, f * P : (f + 1) * P],
+                    nodes[:].indirect(offsets[:, piece * cols : (piece + 1) * cols]),
+                    start=True,
+                    stop=True,
+                )
+                if k == 0:
+                    nc.scalar.copy(best[f, h][:], product[:])
+                else:
+                    nc.vector.tensor_tensor(best[f, h][:], product[:], best[f, h][:], MAX)
 
         wa_neg = held.tile([P, FEATURES], BF16, name="wa_neg")
-        nc.vector.tensor_scalar_mul(wa_neg[:], wa_sb[:], -1.0)
+        nc.gpsimd.tensor_scalar_mul(wa_neg[:], wa_sb[:], -1.0)
 
-        centre = {}
-        for f in range(blocks):
-            for h in range(halves):
-                centre[f, h] = centres.tile([P, PIECE], F32, name=f"centre{f}{h}")
-                here = nodes[:, h * PIECE : (h + 1) * PIECE]
-                feats = slice(f * P, (f + 1) * P)
-                nc.tensor.matmul(centre[f, h][:], wb_sb[:, feats], here, start=True, stop=False)
-                nc.tensor.matmul(centre[f, h][:], wa_neg[:, feats], here, start=False, stop=True)
-
-        for f in range(blocks):
-            for h in range(halves):
-                best = work.tile([P, PIECE], F32, name="best")
-                for k in range(NEIGHBOURS):
-                    piece = k * halves + h
-                    product = products.tile([P, PIECE], F32, name="product")
-                    nc.tensor.matmul(
-                        product[:],
-                        wa_sb[:, f * P : (f + 1) * P],
-                        nodes[:].indirect(offsets[:, piece * cols : (piece + 1) * cols]),
-                        start=True,
-                        stop=True,
-                    )
-                    if k == 0:
-                        nc.scalar.copy(best[:], product[:])
-                    else:
-                        nc.vector.tensor_tensor(best[:], product[:], best[:], MAX)
-                summed = work.tile([P, PIECE], F32, name="summed")
-                nc.vector.scalar_tensor_tensor(summed[:], centre[f, h][:], bias[f][:], best[:], ADD, ADD)
-                result = work.tile([P, PIECE], F32, name="result")
-                nc.vector.scalar_tensor_tensor(result[:], summed[:], SLOPE, summed[:], MULT, MAX)
-                nc.sync.dma_start(out[f * P : (f + 1) * P, h * PIECE : (h + 1) * PIECE], result[:])
+        for f, h in units:
+            here = nodes[:, h * PIECE : (h + 1) * PIECE]
+            feats = slice(f * P, (f + 1) * P)
+            centre = psum.tile([P, PIECE], F32, name="centre", tag="bank")
+            nc.tensor.matmul(centre[:], wb_sb[:, feats], here, start=True, stop=False)
+            nc.tensor.matmul(centre[:], wa_neg[:, feats], here, start=False, stop=True)
+            summed = work.tile([P, PIECE], F32, name="summed")
+            nc.vector.scalar_tensor_tensor(summed[:], centre[:], bias[f][:], best[f, h][:], ADD, ADD)
+            result = work.tile([P, PIECE], F32, name="result")
+            nc.vector.scalar_tensor_tensor(result[:], summed[:], SLOPE, summed[:], MULT, MAX)
+            nc.sync.dma_start(out[f * P : (f + 1) * P, h * PIECE : (h + 1) * PIECE], result[:])

@@ -9,62 +9,85 @@ FEATURES = 256
 NEIGHBOURS = 4
 PIECE = 512
 SLOPE = 0.2
+WARM_UP = 3
 
 FLOPS = 2 * P * FEATURES * (NEIGHBOURS * NODES + 2 * NODES)
 
 
 def tile_skeletonconv_kernel(tc, x, wa, wb, b, offs, out):
     nc = tc.nc
-    cols = PIECE // 16
+    blocks = range(FEATURES // P)
     halves = NODES // PIECE
-    units = [(f, h) for f in range(FEATURES // P) for h in range(halves)]
+    cols = PIECE // 16
 
     with (
         tc.tile_pool(name="held", bufs=1) as held,
-        tc.tile_pool(name="work", bufs=2) as work,
-        tc.psum_pool(name="psum", bufs=8) as psum,
+        tc.tile_pool(name="work", bufs=halves) as work,
+        tc.psum_pool(name="centres", bufs=2) as centres,
+        tc.psum_pool(name="products", bufs=6) as products,
     ):
         offsets = held.tile([P, NEIGHBOURS * NODES // 16], U16, name="offsets")
         nodes = held.tile([P, NODES], BF16, name="nodes")
         wb_sb = held.tile([P, FEATURES], BF16, name="wb_sb")
         wa_sb = held.tile([P, FEATURES], BF16, name="wa_sb")
-        bias = [held.tile([P, 1], F32, name=f"bias{f}") for f in range(FEATURES // P)]
-        nc.sync.dma_start(nodes[:], x)
+        bias = [held.tile([P, 1], F32, name=f"bias{f}") for f in blocks]
+        nc.sync.dma_start(nodes[:, :PIECE], x[:, :PIECE])
         nc.scalar.dma_start(wa_sb[:], wa)
-        nc.sync.dma_start(offsets[:], offs)
         nc.scalar.dma_start(wb_sb[:], wb)
-        for f in range(FEATURES // P):
+        nc.sync.dma_start(nodes[:, PIECE:], x[:, PIECE:])
+        nc.sync.dma_start(offsets[:], offs)
+        for f in blocks:
             nc.scalar.dma_start(bias[f][:], b[f * P : (f + 1) * P, :])
 
-        best = {}
-        for f, h in units:
-            best[f, h] = held.tile([P, PIECE], F32, name=f"best{f}{h}")
-            for k in range(NEIGHBOURS):
-                piece = k * halves + h
-                product = psum.tile([P, PIECE], F32, name="product", tag="bank")
-                nc.tensor.matmul(
-                    product[:],
-                    wa_sb[:, f * P : (f + 1) * P],
-                    nodes[:].indirect(offsets[:, piece * cols : (piece + 1) * cols]),
-                    start=True,
-                    stop=True,
-                )
-                if k == 0:
-                    nc.scalar.copy(best[f, h][:], product[:])
-                else:
-                    nc.vector.tensor_tensor(best[f, h][:], product[:], best[f, h][:], MAX)
+        zeros = held.tile([P, PIECE], BF16, name="zeros")
+        nc.vector.memset(zeros[:], 0.0)
+        warm_up = products.tile([P, PIECE], F32, name="warm_up", tag="product")
+        for i in range(WARM_UP):
+            nc.tensor.matmul(warm_up[:], zeros[:, :P], zeros[:], start=True, stop=True)
 
         wa_neg = held.tile([P, FEATURES], BF16, name="wa_neg")
-        nc.gpsimd.tensor_scalar_mul(wa_neg[:], wa_sb[:], -1.0)
+        nc.vector.tensor_scalar_mul(wa_neg[:], wa_sb[:], -1.0)
 
-        for f, h in units:
+        def centre_terms(h):
             here = nodes[:, h * PIECE : (h + 1) * PIECE]
-            feats = slice(f * P, (f + 1) * P)
-            centre = psum.tile([P, PIECE], F32, name="centre", tag="bank")
-            nc.tensor.matmul(centre[:], wb_sb[:, feats], here, start=True, stop=False)
-            nc.tensor.matmul(centre[:], wa_neg[:, feats], here, start=False, stop=True)
-            summed = work.tile([P, PIECE], F32, name="summed")
-            nc.vector.scalar_tensor_tensor(summed[:], centre[:], bias[f][:], best[f, h][:], ADD, ADD)
-            result = work.tile([P, PIECE], F32, name="result")
-            nc.vector.scalar_tensor_tensor(result[:], summed[:], SLOPE, summed[:], MULT, MAX)
-            nc.sync.dma_start(out[f * P : (f + 1) * P, h * PIECE : (h + 1) * PIECE], result[:])
+            terms = []
+            for f in blocks:
+                feats = slice(f * P, (f + 1) * P)
+                centre = centres.tile([P, PIECE], F32, name="centre")
+                nc.tensor.matmul(centre[:], wb_sb[:, feats], here, start=True, stop=False)
+                nc.tensor.matmul(centre[:], wa_neg[:, feats], here, start=False, stop=True)
+                terms.append(centre)
+            return terms
+
+        def best_neighbours(h):
+            best = [work.tile([P, PIECE], F32, name=f"best{f}") for f in blocks]
+            for k in range(NEIGHBOURS):
+                piece = k * halves + h
+                for f in blocks:
+                    product = products.tile([P, PIECE], F32, name="product")
+                    nc.tensor.matmul(
+                        product[:],
+                        wa_sb[:, f * P : (f + 1) * P],
+                        nodes[:].indirect(offsets[:, piece * cols : (piece + 1) * cols]),
+                        start=True,
+                        stop=True,
+                    )
+                    if k == 0:
+                        nc.scalar.copy(best[f][:], product[:])
+                    else:
+                        nc.vector.tensor_tensor(best[f][:], product[:], best[f][:], MAX)
+            return best
+
+        def finish(h, centre, best):
+            summed = [work.tile([P, PIECE], F32, name=f"summed{f}") for f in blocks]
+            for f in blocks:
+                nc.vector.scalar_tensor_tensor(summed[f][:], centre[f][:], bias[f][:], best[f][:], ADD, ADD)
+            for f, queue in zip(blocks, (nc.sync, nc.scalar)):
+                result = work.tile([P, PIECE], F32, name=f"result{f}")
+                nc.vector.scalar_tensor_tensor(result[:], summed[f][:], SLOPE, summed[f][:], MULT, MAX)
+                queue.dma_start(out[f * P : (f + 1) * P, h * PIECE : (h + 1) * PIECE], result[:])
+
+        centre = centre_terms(0)
+        finish(0, centre, best_neighbours(0))
+        best = best_neighbours(1)
+        finish(1, centre_terms(1), best)

@@ -9,7 +9,6 @@ FEATURES = 256
 NEIGHBOURS = 4
 PIECE = 512
 SLOPE = 0.2
-WARM_UP = 3
 
 FLOPS = 2 * P * FEATURES * (NEIGHBOURS * NODES + 2 * NODES)
 
@@ -38,12 +37,6 @@ def tile_skeletonconv_kernel(tc, x, wa, wb, b, offs, out):
         nc.sync.dma_start(offsets[:], offs)
         for f in blocks:
             nc.scalar.dma_start(bias[f][:], b[f * P : (f + 1) * P, :])
-
-        zeros = held.tile([P, PIECE], BF16, name="zeros")
-        nc.vector.memset(zeros[:], 0.0)
-        warm_up = products.tile([P, PIECE], F32, name="warm_up", tag="product")
-        for i in range(WARM_UP):
-            nc.tensor.matmul(warm_up[:], zeros[:, :P], zeros[:], start=True, stop=True)
 
         wa_neg = held.tile([P, FEATURES], BF16, name="wa_neg")
         nc.vector.tensor_scalar_mul(wa_neg[:], wa_sb[:], -1.0)

@@ -2,6 +2,7 @@ import concourse.mybir as mybir
 
 BF16, F32, U16 = mybir.dt.bfloat16, mybir.dt.float32, mybir.dt.uint16
 ADD, MULT, MAX = mybir.AluOpType.add, mybir.AluOpType.mult, mybir.AluOpType.max
+IDENTITY, RELU = mybir.ActivationFunctionType.Identity, mybir.ActivationFunctionType.Relu
 
 P = 128
 NODES = 1024
@@ -9,6 +10,7 @@ FEATURES = 256
 NEIGHBOURS = 4
 PIECE = 512
 SLOPE = 0.2
+WARM_UP = 3
 
 FLOPS = 2 * P * FEATURES * (NEIGHBOURS * NODES + 2 * NODES)
 
@@ -22,8 +24,7 @@ def tile_skeletonconv_kernel(tc, x, wa, wb, b, offs, out):
     with (
         tc.tile_pool(name="held", bufs=1) as held,
         tc.tile_pool(name="work", bufs=halves) as work,
-        tc.psum_pool(name="centres", bufs=2) as centres,
-        tc.psum_pool(name="products", bufs=6) as products,
+        tc.psum_pool(name="psum", bufs=8) as psum,
     ):
         offsets = held.tile([P, NEIGHBOURS * NODES // 16], U16, name="offsets")
         nodes = held.tile([P, NODES], BF16, name="nodes")
@@ -38,6 +39,12 @@ def tile_skeletonconv_kernel(tc, x, wa, wb, b, offs, out):
         for f in blocks:
             nc.scalar.dma_start(bias[f][:], b[f * P : (f + 1) * P, :])
 
+        zeros = held.tile([P, PIECE], BF16, name="zeros")
+        nc.vector.memset(zeros[:], 0.0)
+        warm_up = psum.tile([P, PIECE], F32, name="warm_up", tag="bank")
+        for i in range(WARM_UP):
+            nc.tensor.matmul(warm_up[:], zeros[:, :P], zeros[:], start=True, stop=True)
+
         wa_neg = held.tile([P, FEATURES], BF16, name="wa_neg")
         nc.vector.tensor_scalar_mul(wa_neg[:], wa_sb[:], -1.0)
 
@@ -46,7 +53,7 @@ def tile_skeletonconv_kernel(tc, x, wa, wb, b, offs, out):
             terms = []
             for f in blocks:
                 feats = slice(f * P, (f + 1) * P)
-                centre = centres.tile([P, PIECE], F32, name="centre")
+                centre = psum.tile([P, PIECE], F32, name="centre", tag="bank")
                 nc.tensor.matmul(centre[:], wb_sb[:, feats], here, start=True, stop=False)
                 nc.tensor.matmul(centre[:], wa_neg[:, feats], here, start=False, stop=True)
                 terms.append(centre)
@@ -57,7 +64,7 @@ def tile_skeletonconv_kernel(tc, x, wa, wb, b, offs, out):
             for k in range(NEIGHBOURS):
                 piece = k * halves + h
                 for f in blocks:
-                    product = products.tile([P, PIECE], F32, name="product")
+                    product = psum.tile([P, PIECE], F32, name="product", tag="bank")
                     nc.tensor.matmul(
                         product[:],
                         wa_sb[:, f * P : (f + 1) * P],
@@ -80,7 +87,25 @@ def tile_skeletonconv_kernel(tc, x, wa, wb, b, offs, out):
                 nc.vector.scalar_tensor_tensor(result[:], summed[f][:], SLOPE, summed[f][:], MULT, MAX)
                 queue.dma_start(out[f * P : (f + 1) * P, h * PIECE : (h + 1) * PIECE], result[:])
 
-        centre = centre_terms(0)
-        finish(0, centre, best_neighbours(0))
-        best = best_neighbours(1)
-        finish(1, centre_terms(1), best)
+        def to_sbuf(centre):
+            moved = [work.tile([P, PIECE], F32, name=f"moved{f}") for f in blocks]
+            for f in blocks:
+                nc.scalar.activation(moved[f][:], centre[f][:], IDENTITY, bias=bias[f][:])
+            return moved
+
+        def finish_aside(h, moved, best):
+            summed = [work.tile([P, PIECE], F32, name=f"summed{f}") for f in blocks]
+            for f in blocks:
+                nc.gpsimd.tensor_tensor(summed[f][:], best[f][:], moved[f][:], ADD)
+            for f in blocks:
+                lift = work.tile([P, PIECE], F32, name=f"lift{f}")
+                nc.scalar.activation(lift[:], summed[f][:], RELU, scale=SLOPE - 1.0)
+                result = work.tile([P, PIECE], F32, name=f"result{f}")
+                nc.gpsimd.tensor_tensor(result[:], summed[f][:], lift[:], ADD)
+                nc.sync.dma_start(out[f * P : (f + 1) * P, h * PIECE : (h + 1) * PIECE], result[:])
+
+        moved = to_sbuf(centre_terms(0))
+        best_first = best_neighbours(0)
+        best_second = best_neighbours(1)
+        finish_aside(0, moved, best_first)
+        finish(1, centre_terms(1), best_second)

@@ -2,14 +2,17 @@ import concourse.mybir as mybir
 
 BF16, F32, U16 = mybir.dt.bfloat16, mybir.dt.float32, mybir.dt.uint16
 ADD, MULT, MAX = mybir.AluOpType.add, mybir.AluOpType.mult, mybir.AluOpType.max
-IDENTITY, RELU = mybir.ActivationFunctionType.Identity, mybir.ActivationFunctionType.Relu
+RELU = mybir.ActivationFunctionType.Relu
 
 P = 128
 NODES = 1024
 FEATURES = 256
 NEIGHBOURS = 4
-PIECE = 512
 SLOPE = 0.2
+PIECE = 512
+HALVES = NODES // PIECE
+BLOCKS = FEATURES // P
+PSUM_BANKS = 8
 WARM_UP = 3
 
 FLOPS = 2 * P * FEATURES * (NEIGHBOURS * NODES + 2 * NODES)
@@ -17,26 +20,24 @@ FLOPS = 2 * P * FEATURES * (NEIGHBOURS * NODES + 2 * NODES)
 
 def tile_skeletonconv_kernel(tc, x, wa, wb, b, offs, out):
     nc = tc.nc
-    blocks = range(FEATURES // P)
-    halves = NODES // PIECE
     cols = PIECE // 16
 
     with (
         tc.tile_pool(name="held", bufs=1) as held,
-        tc.tile_pool(name="work", bufs=halves) as work,
-        tc.psum_pool(name="psum", bufs=8) as psum,
+        tc.tile_pool(name="work", bufs=HALVES) as work,
+        tc.psum_pool(name="psum", bufs=PSUM_BANKS) as psum,
     ):
         offsets = held.tile([P, NEIGHBOURS * NODES // 16], U16, name="offsets")
         nodes = held.tile([P, NODES], BF16, name="nodes")
-        wb_sb = held.tile([P, FEATURES], BF16, name="wb_sb")
         wa_sb = held.tile([P, FEATURES], BF16, name="wa_sb")
-        bias = [held.tile([P, 1], F32, name=f"bias{f}") for f in blocks]
+        wb_sb = held.tile([P, FEATURES], BF16, name="wb_sb")
+        bias = [held.tile([P, 1], F32, name=f"bias{f}") for f in range(BLOCKS)]
         nc.sync.dma_start(nodes[:, :PIECE], x[:, :PIECE])
         nc.scalar.dma_start(wa_sb[:], wa)
         nc.scalar.dma_start(wb_sb[:], wb)
         nc.sync.dma_start(nodes[:, PIECE:], x[:, PIECE:])
         nc.sync.dma_start(offsets[:], offs)
-        for f in blocks:
+        for f in range(BLOCKS):
             nc.scalar.dma_start(bias[f][:], b[f * P : (f + 1) * P, :])
 
         zeros = held.tile([P, PIECE], BF16, name="zeros")
@@ -50,20 +51,20 @@ def tile_skeletonconv_kernel(tc, x, wa, wb, b, offs, out):
 
         def centre_terms(h):
             here = nodes[:, h * PIECE : (h + 1) * PIECE]
-            terms = []
-            for f in blocks:
+            centres = []
+            for f in range(BLOCKS):
                 feats = slice(f * P, (f + 1) * P)
                 centre = psum.tile([P, PIECE], F32, name="centre", tag="bank")
                 nc.tensor.matmul(centre[:], wb_sb[:, feats], here, start=True, stop=False)
                 nc.tensor.matmul(centre[:], wa_neg[:, feats], here, start=False, stop=True)
-                terms.append(centre)
-            return terms
+                centres.append(centre)
+            return centres
 
         def best_neighbours(h):
-            best = [work.tile([P, PIECE], F32, name=f"best{f}") for f in blocks]
+            bests = [work.tile([P, PIECE], F32, name=f"best{f}") for f in range(BLOCKS)]
             for k in range(NEIGHBOURS):
-                piece = k * halves + h
-                for f in blocks:
+                piece = k * HALVES + h
+                for f in range(BLOCKS):
                     product = psum.tile([P, PIECE], F32, name="product", tag="bank")
                     nc.tensor.matmul(
                         product[:],
@@ -73,39 +74,35 @@ def tile_skeletonconv_kernel(tc, x, wa, wb, b, offs, out):
                         stop=True,
                     )
                     if k == 0:
-                        nc.scalar.copy(best[f][:], product[:])
+                        nc.scalar.copy(bests[f][:], product[:])
                     else:
-                        nc.vector.tensor_tensor(best[f][:], product[:], best[f][:], MAX)
-            return best
+                        nc.vector.tensor_tensor(bests[f][:], product[:], bests[f][:], MAX)
+            return bests
 
-        def finish(h, centre, best):
-            summed = [work.tile([P, PIECE], F32, name=f"summed{f}") for f in blocks]
-            for f in blocks:
-                nc.vector.scalar_tensor_tensor(summed[f][:], centre[f][:], bias[f][:], best[f][:], ADD, ADD)
-            for f, queue in zip(blocks, (nc.sync, nc.scalar)):
+        def add_centres(centres, bests):
+            sums = [work.tile([P, PIECE], F32, name=f"summed{f}") for f in range(BLOCKS)]
+            for f in range(BLOCKS):
+                nc.vector.scalar_tensor_tensor(sums[f][:], centres[f][:], bias[f][:], bests[f][:], ADD, ADD)
+            return sums
+
+        def store(queue, f, h, result):
+            queue.dma_start(out[f * P : (f + 1) * P, h * PIECE : (h + 1) * PIECE], result[:])
+
+        def leaky(h, sums):
+            for f, queue in zip(range(BLOCKS), (nc.sync, nc.scalar)):
                 result = work.tile([P, PIECE], F32, name=f"result{f}")
-                nc.vector.scalar_tensor_tensor(result[:], summed[f][:], SLOPE, summed[f][:], MULT, MAX)
-                queue.dma_start(out[f * P : (f + 1) * P, h * PIECE : (h + 1) * PIECE], result[:])
+                nc.vector.scalar_tensor_tensor(result[:], sums[f][:], SLOPE, sums[f][:], MULT, MAX)
+                store(queue, f, h, result)
 
-        def to_sbuf(centre):
-            moved = [work.tile([P, PIECE], F32, name=f"moved{f}") for f in blocks]
-            for f in blocks:
-                nc.scalar.activation(moved[f][:], centre[f][:], IDENTITY, bias=bias[f][:])
-            return moved
-
-        def finish_aside(h, moved, best):
-            summed = [work.tile([P, PIECE], F32, name=f"summed{f}") for f in blocks]
-            for f in blocks:
-                nc.gpsimd.tensor_tensor(summed[f][:], best[f][:], moved[f][:], ADD)
-            for f in blocks:
+        def leaky_aside(h, sums):
+            for f in range(BLOCKS):
                 lift = work.tile([P, PIECE], F32, name=f"lift{f}")
-                nc.scalar.activation(lift[:], summed[f][:], RELU, scale=SLOPE - 1.0)
+                nc.scalar.activation(lift[:], sums[f][:], RELU, scale=SLOPE - 1.0)
                 result = work.tile([P, PIECE], F32, name=f"result{f}")
-                nc.gpsimd.tensor_tensor(result[:], summed[f][:], lift[:], ADD)
-                nc.sync.dma_start(out[f * P : (f + 1) * P, h * PIECE : (h + 1) * PIECE], result[:])
+                nc.gpsimd.tensor_tensor(result[:], sums[f][:], lift[:], ADD)
+                store(nc.sync, f, h, result)
 
-        moved = to_sbuf(centre_terms(0))
-        best_first = best_neighbours(0)
-        best_second = best_neighbours(1)
-        finish_aside(0, moved, best_first)
-        finish(1, centre_terms(1), best_second)
+        sums_first = add_centres(centre_terms(0), best_neighbours(0))
+        bests_second = best_neighbours(1)
+        leaky_aside(0, sums_first)
+        leaky(1, add_centres(centre_terms(1), bests_second))

@@ -13,6 +13,7 @@ PIECE = 512
 HALVES = NODES // PIECE
 BLOCKS = FEATURES // P
 PSUM_BANKS = 8
+CUTS = 2
 WARM_UP = 3
 
 FLOPS = 2 * P * FEATURES * (NEIGHBOURS * NODES + 2 * NODES)
@@ -89,10 +90,16 @@ def tile_skeletonconv_kernel(tc, x, wa, wb, b, offs, out):
             queue.dma_start(out[f * P : (f + 1) * P, h * PIECE : (h + 1) * PIECE], result[:])
 
         def leaky(h, sums):
-            for f, queue in zip(range(BLOCKS), (nc.sync, nc.scalar)):
+            width = PIECE // CUTS
+            queues = (nc.sync, nc.scalar)
+            for f in range(BLOCKS):
                 result = work.tile([P, PIECE], F32, name=f"result{f}")
-                nc.vector.scalar_tensor_tensor(result[:], sums[f][:], SLOPE, sums[f][:], MULT, MAX)
-                store(queue, f, h, result)
+                for c in range(CUTS):
+                    cut = slice(c * width, (c + 1) * width)
+                    nc.vector.scalar_tensor_tensor(result[:, cut], sums[f][:, cut], SLOPE, sums[f][:, cut], MULT, MAX)
+                    queues[c % 2].dma_start(
+                        out[f * P : (f + 1) * P, h * PIECE + cut.start : h * PIECE + cut.stop], result[:, cut]
+                    )
 
         def leaky_aside(h, sums):
             for f in range(BLOCKS):

@@ -35,7 +35,7 @@ def tile_skeletonconv_kernel(tc, x, wa, wb, b, offs, out):
         bias = [held.tile([P, 1], F32, name=f"bias{f}") for f in range(BLOCKS)]
         nc.sync.dma_start(nodes[:, :PIECE], x[:, :PIECE])
         nc.scalar.dma_start(wa_sb[:], wa)
-        nc.scalar.dma_start(wb_sb[:], wb)
+        nc.sync.dma_start(wb_sb[:], wb)
         nc.sync.dma_start(nodes[:, PIECE:], x[:, PIECE:])
         nc.sync.dma_start(offsets[:], offs)
         for f in range(BLOCKS):

@@ -34,8 +34,8 @@ def tile_skeletonconv_kernel(tc, x, wa, wb, b, offs, out):
         wb_sb = held.tile([P, FEATURES], BF16, name="wb_sb")
         bias = [held.tile([P, 1], F32, name=f"bias{f}") for f in range(BLOCKS)]
         nc.sync.dma_start(nodes[:, :PIECE], x[:, :PIECE])
-        nc.scalar.dma_start(wa_sb[:], wa)
-        nc.sync.dma_start(wb_sb[:], wb)
+        nc.scalar.dma_start(wb_sb[:], wb)
+        nc.sync.dma_start(wa_sb[:], wa)
         nc.sync.dma_start(nodes[:, PIECE:], x[:, PIECE:])
         nc.sync.dma_start(offsets[:], offs)
         for f in range(BLOCKS):
@@ -52,13 +52,11 @@ def tile_skeletonconv_kernel(tc, x, wa, wb, b, offs, out):
 
         def centre_terms(h):
             here = nodes[:, h * PIECE : (h + 1) * PIECE]
-            centres = []
+            centres = [psum.tile([P, PIECE], F32, name=f"centre{f}", tag="bank") for f in range(BLOCKS)]
             for f in range(BLOCKS):
-                feats = slice(f * P, (f + 1) * P)
-                centre = psum.tile([P, PIECE], F32, name="centre", tag="bank")
-                nc.tensor.matmul(centre[:], wb_sb[:, feats], here, start=True, stop=False)
-                nc.tensor.matmul(centre[:], wa_neg[:, feats], here, start=False, stop=True)
-                centres.append(centre)
+                nc.tensor.matmul(centres[f][:], wb_sb[:, f * P : (f + 1) * P], here, start=True, stop=False)
+            for f in range(BLOCKS):
+                nc.tensor.matmul(centres[f][:], wa_neg[:, f * P : (f + 1) * P], here, start=False, stop=True)
             return centres
 
         def best_neighbours(h):

@@ -14,7 +14,7 @@ HALVES = NODES // PIECE
 BLOCKS = FEATURES // P
 PSUM_BANKS = 8
 CUTS = 2
-WARM_UP = 3
+WARM_UP = 2
 
 FLOPS = 2 * P * FEATURES * (NEIGHBOURS * NODES + 2 * NODES)
 

@@ -14,7 +14,7 @@ HALVES = NODES // PIECE
 BLOCKS = FEATURES // P
 PSUM_BANKS = 8
 CUTS = 2
-WARM_UP = 2
+WARM_UP = 8
 
 FLOPS = 2 * P * FEATURES * (NEIGHBOURS * NODES + 2 * NODES)
 
@@ -41,11 +41,11 @@ def tile_skeletonconv_kernel(tc, x, wa, wb, b, offs, out):
         for f in range(BLOCKS):
             nc.scalar.dma_start(bias[f][:], b[f * P : (f + 1) * P, :])
 
-        zeros = held.tile([P, PIECE], BF16, name="zeros")
+        zeros = held.tile([P, P], BF16, name="zeros")
         nc.vector.memset(zeros[:], 0.0)
-        warm_up = psum.tile([P, PIECE], F32, name="warm_up", tag="bank")
+        warm_up = psum.tile([P, P], F32, name="warm_up", tag="bank")
         for i in range(WARM_UP):
-            nc.tensor.matmul(warm_up[:], zeros[:, :P], zeros[:], start=True, stop=True)
+            nc.tensor.matmul(warm_up[:], zeros[:], zeros[:], start=True, stop=True)
 
         wa_neg = held.tile([P, FEATURES], BF16, name="wa_neg")
         nc.vector.tensor_scalar_mul(wa_neg[:], wa_sb[:], -1.0)

import concourse.mybir as mybir

BF16, F32, U16 = mybir.dt.bfloat16, mybir.dt.float32, mybir.dt.uint16
ADD, MULT, MAX = mybir.AluOpType.add, mybir.AluOpType.mult, mybir.AluOpType.max
RELU = mybir.ActivationFunctionType.Relu

P = 128
NODES = 1024
FEATURES = 256
NEIGHBOURS = 4
SLOPE = 0.2
PIECE = 512
HALVES = NODES // PIECE
BLOCKS = FEATURES // P
PSUM_BANKS = 8
CUTS = 2
WARM_UP = 8

FLOPS = 2 * P * FEATURES * (NEIGHBOURS * NODES + 2 * NODES)


def tile_skeletonconv_kernel(tc, x, wa, wb, b, offs, out):
    nc = tc.nc
    cols = PIECE // 16

    with (
        tc.tile_pool(name="held", bufs=1) as held,
        tc.tile_pool(name="work", bufs=HALVES) as work,
        tc.psum_pool(name="psum", bufs=PSUM_BANKS) as psum,
    ):
        offsets = held.tile([P, NEIGHBOURS * NODES // 16], U16, name="offsets")
        nodes = held.tile([P, NODES], BF16, name="nodes")
        wa_sb = held.tile([P, FEATURES], BF16, name="wa_sb")
        wb_sb = held.tile([P, FEATURES], BF16, name="wb_sb")
        bias = [held.tile([P, 1], F32, name=f"bias{f}") for f in range(BLOCKS)]
        nc.sync.dma_start(nodes[:, :PIECE], x[:, :PIECE])
        nc.scalar.dma_start(wb_sb[:], wb)
        nc.sync.dma_start(wa_sb[:], wa)
        nc.sync.dma_start(nodes[:, PIECE:], x[:, PIECE:])
        nc.sync.dma_start(offsets[:], offs)
        for f in range(BLOCKS):
            nc.scalar.dma_start(bias[f][:], b[f * P : (f + 1) * P, :])

        zeros = held.tile([P, P], BF16, name="zeros")
        nc.vector.memset(zeros[:], 0.0)
        warm_up = psum.tile([P, P], F32, name="warm_up", tag="bank")
        for i in range(WARM_UP):
            nc.tensor.matmul(warm_up[:], zeros[:], zeros[:], start=True, stop=True)

        wa_neg = held.tile([P, FEATURES], BF16, name="wa_neg")
        nc.vector.tensor_scalar_mul(wa_neg[:], wa_sb[:], -1.0)

        def centre_terms(h):
            here = nodes[:, h * PIECE : (h + 1) * PIECE]
            centres = [psum.tile([P, PIECE], F32, name=f"centre{f}", tag="bank") for f in range(BLOCKS)]
            for f in range(BLOCKS):
                nc.tensor.matmul(centres[f][:], wb_sb[:, f * P : (f + 1) * P], here, start=True, stop=False)
            for f in range(BLOCKS):
                nc.tensor.matmul(centres[f][:], wa_neg[:, f * P : (f + 1) * P], here, start=False, stop=True)
            return centres

        def best_neighbours(h):
            bests = [work.tile([P, PIECE], F32, name=f"best{f}") for f in range(BLOCKS)]
            for k in range(NEIGHBOURS):
                piece = k * HALVES + h
                for f in range(BLOCKS):
                    product = psum.tile([P, PIECE], F32, name="product", tag="bank")
                    nc.tensor.matmul(
                        product[:],
                        wa_sb[:, f * P : (f + 1) * P],
                        nodes[:].indirect(offsets[:, piece * cols : (piece + 1) * cols]),
                        start=True,
                        stop=True,
                    )
                    if k == 0:
                        nc.scalar.copy(bests[f][:], product[:])
                    else:
                        nc.vector.tensor_tensor(bests[f][:], product[:], bests[f][:], MAX)
            return bests

        def add_centres(centres, bests):
            sums = [work.tile([P, PIECE], F32, name=f"summed{f}") for f in range(BLOCKS)]
            for f in range(BLOCKS):
                nc.vector.scalar_tensor_tensor(sums[f][:], centres[f][:], bias[f][:], bests[f][:], ADD, ADD)
            return sums

        def store(queue, f, h, result):
            queue.dma_start(out[f * P : (f + 1) * P, h * PIECE : (h + 1) * PIECE], result[:])

        def leaky(h, sums):
            width = PIECE // CUTS
            queues = (nc.sync, nc.scalar)
            for f in range(BLOCKS):
                result = work.tile([P, PIECE], F32, name=f"result{f}")
                for c in range(CUTS):
                    cut = slice(c * width, (c + 1) * width)
                    nc.vector.scalar_tensor_tensor(result[:, cut], sums[f][:, cut], SLOPE, sums[f][:, cut], MULT, MAX)
                    queues[c % 2].dma_start(
                        out[f * P : (f + 1) * P, h * PIECE + cut.start : h * PIECE + cut.stop], result[:, cut]
                    )

        def leaky_aside(h, sums):
            for f in range(BLOCKS):
                lift = work.tile([P, PIECE], F32, name=f"lift{f}")
                nc.scalar.activation(lift[:], sums[f][:], RELU, scale=SLOPE - 1.0)
                result = work.tile([P, PIECE], F32, name=f"result{f}")
                nc.gpsimd.tensor_tensor(result[:], sums[f][:], lift[:], ADD)
                store(nc.sync, f, h, result)

        sums_first = add_centres(centre_terms(0), best_neighbours(0))
        bests_second = best_neighbours(1)
        leaky_aside(0, sums_first)
        leaky(1, add_centres(centre_terms(1), bests_second))
